import numpy as np
import ml_dtypes


def mxq(x, axis, fmt="e4m3"):
    dtype, down = {"e4m3": (ml_dtypes.float8_e4m3fn, 7), "e5m2": (ml_dtypes.float8_e5m2, 14)}[fmt]
    v = np.moveaxis(np.asarray(x, np.float32).astype(ml_dtypes.bfloat16).astype(np.float64), axis, -1)
    blocks = v.reshape(v.shape[:-1] + (-1, 32))
    amax = np.abs(blocks).max(-1, keepdims=True)
    byte = np.maximum(np.where(amax > 0, np.frexp(amax)[1] - 1 + 127, 0) - down, 1)
    scale = np.exp2(byte - 127.0)
    codes = (blocks / scale).astype(np.float32).astype(dtype).astype(np.float64)
    return np.moveaxis((codes * scale).reshape(v.shape), -1, axis)


WIDE = False


def mx_kscale(k):
    if not WIDE:
        return np.ones(k)
    levels = np.array([10, -10, 5, -5, 0])
    a = np.random.permutation(np.resize(levels, k // 512 * 4)).reshape(k // 512, 4)
    idx = np.arange(k)
    return np.exp2(a[idx // 512, idx % 128 // 32])


BF16 = ml_dtypes.bfloat16


def bf(x):
    return np.asarray(x, np.float32).astype(BF16)


def f64(x):
    return np.asarray(x).astype(np.float64)


E2M1 = np.array([0.0, 0.5, 1.0, 1.5, 2.0, 3.0, 4.0, 6.0, -0.0, -0.5, -1.0, -1.5, -2.0, -3.0, -4.0, -6.0])


def pack_weight(w, fmt):
    k, n = w.shape
    w = f64(bf(w)).reshape(k // 32, 32, n)
    amax = np.abs(w).max(1)
    if fmt == "e4m3":
        byte = np.frexp(amax)[1] - 1 + 127 - 7
    else:
        mant, ex = np.frexp(amax / 6.0)
        byte = np.where(mant > 0.5, ex, ex - 1) + 127
    byte = np.clip(np.where(amax > 0, byte, 1), 1, 254)
    scaled = (w * np.exp2(127.0 - byte)[:, None, :]).reshape(k, n).astype(np.float32)
    by_word = np.ascontiguousarray(scaled.reshape(k // 512, 128, 4, n).transpose(0, 1, 3, 2))
    if fmt == "e4m3":
        words = by_word.astype(ml_dtypes.float8_e4m3fn).view(np.uint8)
    else:
        c = by_word.astype(ml_dtypes.float4_e2m1fn).view(np.uint8) & 0xF
        words = c[..., 0::2] | (c[..., 1::2] << 4)
    return np.ascontiguousarray(words), np.ascontiguousarray(byte.astype(np.uint8).reshape(k // 512, 16, n))


def unpack_weight(words, scales, fmt):
    g, p, n, _ = words.shape
    if fmt == "e4m3":
        vals = np.ascontiguousarray(words).view(ml_dtypes.float8_e4m3fn).astype(np.float64)
    else:
        nib = np.empty((g, p, n, 4), np.uint8)
        nib[..., 0::2] = words & 0xF
        nib[..., 1::2] = words >> 4
        vals = E2M1[nib]
    vals = vals * np.repeat(np.exp2(scales.astype(np.float64) - 127.0), 8, axis=1)[..., None]
    return vals.transpose(0, 1, 3, 2).reshape(g * 512, n)


B, C, H, W, HEADS, HD = 16, 512, 16, 16, 2, 512
N = H * W


def setup_inputs():
    t = mx_kscale(HD)
    x = bf(np.random.standard_normal((B, C, H, W)))
    q_w = np.random.standard_normal((HEADS, HD, C)) * 0.5 / np.sqrt(C) * t[None, :, None]
    q_b = bf(np.random.standard_normal((HEADS, HD)) * 4.0 / N * t)
    k_w = np.random.standard_normal((HEADS, HD, C)) * 0.5 / np.sqrt(C) / t[None, :, None]
    k_b = bf(np.random.standard_normal((HEADS, HD)) * 0.1 / t)
    q_cat = np.ascontiguousarray(q_w.swapaxes(1, 2)).reshape(-1, HD)
    k_cat = np.ascontiguousarray(k_w.swapaxes(1, 2)).reshape(-1, HD)
    q_w_words, q_w_scales = pack_weight(q_cat, "e4m3")
    k_w_words, k_w_scales = pack_weight(k_cat, "e4m3")
    return {"x": x,
            "q_w_words": q_w_words, "q_w_scales": q_w_scales,
            "q_b": q_b,
            "k_w_words": k_w_words, "k_w_scales": k_w_scales,
            "k_b": k_b}


def reference(x, q_w_words, q_w_scales, q_b, k_w_words, k_w_scales, k_b):
    x = f64(x)
    patch = x.transpose(0, 2, 3, 1).reshape(B, N, C)
    pq = mxq(patch, 2, "e4m3")[:, None]
    Q = (pq @ unpack_weight(q_w_words, q_w_scales, "e4m3").reshape(HEADS, C, HD)[None]) + f64(q_b)[None, :, None, :]
    K = (pq @ unpack_weight(k_w_words, k_w_scales, "e4m3").reshape(HEADS, C, HD)[None]) + f64(k_b)[None, :, None, :]
    sim = (mxq(Q, 3, "e4m3") @ mxq(K, 3, "e4m3").transpose(0, 1, 3, 2)) / np.sqrt(HD)
    att = sim.sum(axis=2)[:, :, None, :]
    e = np.exp(att - att.max(axis=1, keepdims=True))
    att = e / e.sum(axis=1, keepdims=True)
    attention_score = att.reshape(B, HEADS, H, W)
    x_enhance = (attention_score[:, :, None, :, :] * x[:, None, :, :, :]).reshape(B, HEADS * C, H, W)
    return (attention_score, x_enhance, sim)

@@ -1,0 +1,226 @@
+import math
+from contextlib import ExitStack
+
+import concourse.mybir as mybir
+from concourse.masks import make_identity
+
+FP8X4 = mybir.dt.float8_e4m3fn_x4
+BF16 = mybir.dt.bfloat16
+F32 = mybir.dt.float32
+I32 = mybir.dt.int32
+U32 = mybir.dt.uint32
+U8 = mybir.dt.uint8
+ACT = mybir.ActivationFunctionType
+ALU = mybir.AluOpType
+
+P = 128
+PACK = 4
+B = 16
+C = 512
+N = 256
+HEADS = 2
+HD = 512
+N_TILES = N // P
+Q_SIDE, K_SIDE = 0, 1
+INV_SQRT_HD = 1.0 / math.sqrt(HD)
+
+FLOPS = 2 * B * HEADS * N * C * HD * 2 + 2 * B * HEADS * N * N * HD
+
+
+def tile_acd_pa_t_e_kernel(
+    tc, x, q_w_words, q_w_scales, q_b, k_w_words, k_w_scales, k_b, out_0, out_1, out_2
+):
+    nc = tc.nc
+    with ExitStack() as ctx:
+        keep = ctx.enter_context(tc.tile_pool(name="keep", bufs=1))
+        stage = ctx.enter_context(tc.tile_pool(name="stage", bufs=2))
+        results = ctx.enter_context(tc.tile_pool(name="results", bufs=3))
+        proj_psum = ctx.enter_context(tc.psum_pool(name="proj_psum", bufs=5))
+        sim_psum = ctx.enter_context(tc.psum_pool(name="sim_psum", bufs=2))
+        gate_psum = ctx.enter_context(tc.psum_pool(name="gate_psum", bufs=1))
+        ctx.enter_context(tc.manual_schedule())
+
+        x_sb = keep.tile([P, B, PACK, N], BF16)
+        w_words = keep.tile([P, 2, HEADS, HD], U32, align_bytes=64)
+        w_scales = keep.tile([P, 2, HEADS, HD], U8, align_bytes=64)
+        bias_rows = keep.tile([P, P], BF16)
+        identity = keep.tile([P, P], BF16)
+        bias = keep.tile([P, 2 * HEADS * PACK], F32)
+        plus_ones = keep.tile([P, P], F32)
+        minus_ones = keep.tile([P, P], F32)
+
+        nc.vector.memset(w_scales[:].rearrange("p s h d -> p (s h d)").bitcast(I32), 0)
+        nc.vector.memset(bias_rows[:], 0.0)
+        nc.vector.memset(plus_ones[:], 1.0)
+        nc.vector.memset(minus_ones[:], -1.0)
+        make_identity(nc, identity[:])
+
+        def load_x(b):
+            nc.sync.dma_start(out=x_sb[:, b], in_=x[b].rearrange("(p j) i w -> p j (i w)", j=PACK))
+
+        def load_weight(side, words, scales):
+            nc.sync.dma_start(
+                out=w_words[:, side].bitcast(I32),
+                in_=words.rearrange("g p d t -> p g (d t)").bitcast(I32),
+            )
+            for quad in range(4):
+                nc.sync.dma_start(
+                    out=w_scales[32 * quad : 32 * quad + 4, side].bitcast(I32),
+                    in_=scales[:, 4 * quad : 4 * quad + 4, :].rearrange("g r d -> r g d").bitcast(I32),
+                )
+
+        load_x(0)
+        load_weight(Q_SIDE, q_w_words, q_w_scales)
+        nc.sync.dma_start(out=bias_rows[0:8, :], in_=q_b.rearrange("h (t p) -> (h t) p", p=P))
+        nc.sync.dma_start(out=bias_rows[8:16, :], in_=k_b.rearrange("h (t p) -> (h t) p", p=P))
+        load_weight(K_SIDE, k_w_words, k_w_scales)
+        for b in range(1, B):
+            load_x(b)
+
+        bias_ps = gate_psum.tile([P, P], BF16, tag="gate")
+        nc.tensor.transpose(bias_ps[:], bias_rows[:], identity[:])
+        nc.vector.tensor_copy(out=bias[:], in_=bias_ps[:, 0 : 2 * HEADS * PACK])
+
+        patch_grouped = {}
+        patch_codes = {}
+        patch_scales = {}
+        qk_grouped = {}
+        qk_codes = {}
+        qk_scales = {}
+        sim_sbs = {}
+        diffs = {}
+
+        def regroup_patch(b):
+            grouped = stage.tile([P, N, PACK], BF16, align_bytes=64, tag="patch_grouped")
+            nc.scalar.copy(out=grouped[:], in_=x_sb[:, b].rearrange("p j n -> p n j"))
+            patch_grouped[b] = grouped
+
+        def quantise_patch(b):
+            codes = stage.tile([P, N], U32, align_bytes=64, tag="patch_codes", bufs=3)
+            scales = stage.tile([P, N], U8, align_bytes=64, tag="patch_scales", bufs=3)
+            nc.vector.quantize_mx(
+                out=codes[:].bitcast(FP8X4),
+                scales=scales[:],
+                in_=patch_grouped[b][:].rearrange("p n j -> p (n j)"),
+            )
+            patch_codes[b] = codes
+            patch_scales[b] = scales
+
+        def open_batch(b):
+            grouped = stage.tile([P, 2, HEADS, N, PACK], BF16, align_bytes=64, tag="qk_grouped")
+            codes = stage.tile([P, 2, HEADS, N], U32, align_bytes=64, tag="qk_codes")
+            scales = stage.tile([P, 2, HEADS, N], U8, align_bytes=64, tag="qk_scales")
+            qk_grouped[b] = grouped
+            qk_codes[b] = codes
+            qk_scales[b] = scales
+
+        def project(b, side, h):
+            first = (side * HEADS + h) * PACK
+            for nt in range(N_TILES):
+                n_cols = slice(nt * P, (nt + 1) * P)
+                acc = proj_psum.tile([P, PACK, P], F32, tag="proj")
+                for t in range(PACK):
+                    d_cols = slice(t * P, (t + 1) * P)
+                    nc.tensor.matmul_mx(
+                        out=acc[:, t, :],
+                        lhsT=w_words[:, side, h, d_cols].bitcast(FP8X4),
+                        lhsT_scale=w_scales[:, side, h, d_cols],
+                        rhs=patch_codes[b][:, n_cols].bitcast(FP8X4),
+                        rhs_scale=patch_scales[b][:, n_cols],
+                        start=True,
+                        stop=True,
+                    )
+                nc.vector.tensor_tensor(
+                    out=qk_grouped[b][:, side, h, n_cols, :],
+                    in0=acc[:].rearrange("p t n -> p n t"),
+                    in1=bias[:, first : first + PACK].unsqueeze(1).to_broadcast([P, P, PACK]),
+                    op=ALU.add,
+                )
+
+        def quantise_side(b, side):
+            nc.vector.quantize_mx(
+                out=qk_codes[b][:, side].rearrange("p h n -> p (h n)").bitcast(FP8X4),
+                scales=qk_scales[b][:, side].rearrange("p h n -> p (h n)"),
+                in_=qk_grouped[b][:, side].rearrange("p h n t -> p (h n t)"),
+            )
+
+        def similarity(b):
+            codes, scales = qk_codes[b], qk_scales[b]
+            sim_sb = results.tile([P, HEADS, N_TILES, N], F32, tag="sim_sb")
+            for h in range(HEADS):
+                sim_ps = sim_psum.tile([P, N_TILES, N], F32, tag="sim")
+                for qt in range(N_TILES):
+                    q_cols = slice(qt * P, (qt + 1) * P)
+                    nc.tensor.matmul_mx(
+                        out=sim_ps[:, qt, :],
+                        lhsT=codes[:, Q_SIDE, h, q_cols].bitcast(FP8X4),
+                        lhsT_scale=scales[:, Q_SIDE, h, q_cols],
+                        rhs=codes[:, K_SIDE, h, :].bitcast(FP8X4),
+                        rhs_scale=scales[:, K_SIDE, h, :],
+                        start=True,
+                        stop=True,
+                    )
+                nc.scalar.activation(out=sim_sb[:, h], in_=sim_ps[:], func=ACT.Copy, scale=INV_SQRT_HD)
+            nc.sync.dma_start(out=out_2[b].rearrange("h (qt p) k -> p h qt k", p=P), in_=sim_sb[:])
+            sim_sbs[b] = sim_sb
+
+        def sum_queries(b, h):
+            if h == 0:
+                diff = gate_psum.tile([P, N], F32, tag="gate")
+                diffs[b] = diff
+            for qt in range(N_TILES):
+                nc.tensor.matmul(
+                    out=diffs[b][:],
+                    lhsT=(plus_ones if h == 0 else minus_ones)[:],
+                    rhs=sim_sbs[b][:, h, qt, :],
+                    start=(h == 0 and qt == 0),
+                    stop=(h == HEADS - 1 and qt == N_TILES - 1),
+                )
+
+        def gate_and_enhance(b):
+            att = results.tile([P, HEADS, N], F32, tag="att")
+            nc.scalar.activation(out=att[:, 0, :], in_=diffs[b][:], func=ACT.Sigmoid, scale=1.0)
+            nc.scalar.activation(out=att[:, 1, :], in_=diffs[b][:], func=ACT.Sigmoid, scale=-1.0)
+            nc.sync.dma_start(
+                out=out_0[b : b + 1].rearrange("o h i w -> o (h i w)"),
+                in_=att[0:1].rearrange("o h n -> o (h n)"),
+            )
+            enhanced = results.tile([P, HEADS, PACK, N], F32, tag="enhanced")
+            for h in range(HEADS):
+                nc.gpsimd.tensor_tensor(
+                    out=enhanced[:, h],
+                    in0=x_sb[:, b],
+                    in1=att[:, h, :].unsqueeze(1).to_broadcast([P, PACK, N]),
+                    op=ALU.mult,
+                )
+            nc.sync.dma_start(
+                out=out_1[b].rearrange("(h p j) i w -> p h (j i w)", h=HEADS, j=PACK),
+                in_=enhanced[:].rearrange("p h j n -> p h (j n)"),
+            )
+
+        for b in range(2):
+            regroup_patch(b)
+            quantise_patch(b)
+        for b in range(B + 1):
+            if b < B:
+                open_batch(b)
+                project(b, Q_SIDE, 0)
+                project(b, Q_SIDE, 1)
+            if b >= 1:
+                similarity(b - 1)
+            if b + 2 < B:
+                regroup_patch(b + 2)
+            if b < B:
+                project(b, K_SIDE, 0)
+                quantise_side(b, Q_SIDE)
+            if b >= 1:
+                sum_queries(b - 1, 0)
+            if b < B:
+                project(b, K_SIDE, 1)
+            if b >= 1:
+                sum_queries(b - 1, 1)
+                gate_and_enhance(b - 1)
+            if b + 2 < B:
+                quantise_patch(b + 2)
+            if b < B:
+                quantise_side(b, K_SIDE)

@@ -212,7 +212,6 @@ def tile_acd_pa_t_e_kernel(
                 regroup_patch(b + 2)
             if b < B:
                 project(b, K_SIDE, 0)
-                quantise_side(b, Q_SIDE)
             if b >= 1:
                 sum_queries(b - 1, 0)
             if b < B:
@@ -220,6 +219,8 @@ def tile_acd_pa_t_e_kernel(
             if b >= 1:
                 sum_queries(b - 1, 1)
                 gate_and_enhance(b - 1)
+            if b < B:
+                quantise_side(b, Q_SIDE)
             if b + 2 < B:
                 quantise_patch(b + 2)
             if b < B:

@@ -70,9 +70,9 @@ def tile_acd_pa_t_e_kernel(
                 )
 
         load_x(0)
-        load_weight(Q_SIDE, q_w_words, q_w_scales)
         nc.sync.dma_start(out=bias_rows[0:8, :], in_=q_b.rearrange("h (t p) -> (h t) p", p=P))
         nc.sync.dma_start(out=bias_rows[8:16, :], in_=k_b.rearrange("h (t p) -> (h t) p", p=P))
+        load_weight(Q_SIDE, q_w_words, q_w_scales)
         load_weight(K_SIDE, k_w_words, k_w_scales)
         for b in range(1, B):
             load_x(b)
@@ -89,6 +89,7 @@ def tile_acd_pa_t_e_kernel(
         qk_scales = {}
         sim_sbs = {}
         diffs = {}
+        atts = {}
 
         def regroup_patch(b):
             grouped = stage.tile([P, N, PACK], BF16, align_bytes=64, tag="patch_grouped")
@@ -177,7 +178,7 @@ def tile_acd_pa_t_e_kernel(
                     stop=(h == HEADS - 1 and qt == N_TILES - 1),
                 )
 
-        def gate_and_enhance(b):
+        def gate(b):
             att = results.tile([P, HEADS, N], F32, tag="att")
             nc.scalar.activation(out=att[:, 0, :], in_=diffs[b][:], func=ACT.Sigmoid, scale=1.0)
             nc.scalar.activation(out=att[:, 1, :], in_=diffs[b][:], func=ACT.Sigmoid, scale=-1.0)
@@ -185,18 +186,20 @@ def tile_acd_pa_t_e_kernel(
                 out=out_0[b : b + 1].rearrange("o h i w -> o (h i w)"),
                 in_=att[0:1].rearrange("o h n -> o (h n)"),
             )
-            enhanced = results.tile([P, HEADS, PACK, N], F32, tag="enhanced")
+            atts[b] = att
+
+        def enhance(b):
+            enhanced_rows = out_1[b].rearrange("(h p j) i w -> h p (j i w)", h=HEADS, j=PACK)
             for h in range(HEADS):
-                nc.gpsimd.tensor_tensor(
-                    out=enhanced[:, h],
+                engine = nc.vector if (h == 1 and b >= B - 2) else nc.gpsimd
+                enhanced = results.tile([P, PACK, N], F32, tag="enhanced", bufs=6)
+                engine.tensor_tensor(
+                    out=enhanced[:],
                     in0=x_sb[:, b],
-                    in1=att[:, h, :].unsqueeze(1).to_broadcast([P, PACK, N]),
+                    in1=atts[b][:, h, :].unsqueeze(1).to_broadcast([P, PACK, N]),
                     op=ALU.mult,
                 )
-            nc.sync.dma_start(
-                out=out_1[b].rearrange("(h p j) i w -> p h (j i w)", h=HEADS, j=PACK),
-                in_=enhanced[:].rearrange("p h j n -> p h (j n)"),
-            )
+                nc.sync.dma_start(out=enhanced_rows[h], in_=enhanced[:].rearrange("p j n -> p (j n)"))
 
         for b in range(2):
             regroup_patch(b)
@@ -218,10 +221,12 @@ def tile_acd_pa_t_e_kernel(
                 project(b, K_SIDE, 1)
             if b >= 1:
                 sum_queries(b - 1, 1)
-                gate_and_enhance(b - 1)
+                gate(b - 1)
             if b < B:
                 quantise_side(b, Q_SIDE)
             if b + 2 < B:
                 quantise_patch(b + 2)
             if b < B:
                 quantise_side(b, K_SIDE)
+            if b >= 1:
+                enhance(b - 1)

@@ -23,6 +23,8 @@ HD = 512
 N_TILES = N // P
 Q_SIDE, K_SIDE = 0, 1
 INV_SQRT_HD = 1.0 / math.sqrt(HD)
+VECTOR_ROWS = 1
+VECTOR_ROWS_AT_END = 3
 
 FLOPS = 2 * B * HEADS * N * C * HD * 2 + 2 * B * HEADS * N * N * HD
 
@@ -35,7 +37,8 @@ def tile_acd_pa_t_e_kernel(
         keep = ctx.enter_context(tc.tile_pool(name="keep", bufs=1))
         stage = ctx.enter_context(tc.tile_pool(name="stage", bufs=2))
         results = ctx.enter_context(tc.tile_pool(name="results", bufs=3))
-        proj_psum = ctx.enter_context(tc.psum_pool(name="proj_psum", bufs=5))
+        proj_psum = ctx.enter_context(tc.psum_pool(name="proj_psum", bufs=3))
+        planes_psum = ctx.enter_context(tc.psum_pool(name="planes_psum", bufs=2))
         sim_psum = ctx.enter_context(tc.psum_pool(name="sim_psum", bufs=2))
         gate_psum = ctx.enter_context(tc.psum_pool(name="gate_psum", bufs=1))
         ctx.enter_context(tc.manual_schedule())
@@ -72,8 +75,8 @@ def tile_acd_pa_t_e_kernel(
         load_x(0)
         nc.sync.dma_start(out=bias_rows[0:8, :], in_=q_b.rearrange("h (t p) -> (h t) p", p=P))
         nc.sync.dma_start(out=bias_rows[8:16, :], in_=k_b.rearrange("h (t p) -> (h t) p", p=P))
-        load_weight(Q_SIDE, q_w_words, q_w_scales)
         load_weight(K_SIDE, k_w_words, k_w_scales)
+        load_weight(Q_SIDE, q_w_words, q_w_scales)
         for b in range(1, B):
             load_x(b)
 
@@ -81,19 +84,30 @@ def tile_acd_pa_t_e_kernel(
         nc.tensor.transpose(bias_ps[:], bias_rows[:], identity[:])
         nc.vector.tensor_copy(out=bias[:], in_=bias_ps[:, 0 : 2 * HEADS * PACK])
 
+        def bias_column(side, h):
+            return (side * HEADS + h) * PACK
+
         patch_grouped = {}
         patch_codes = {}
         patch_scales = {}
+        planes = {}
         qk_grouped = {}
         qk_codes = {}
         qk_scales = {}
         sim_sbs = {}
         diffs = {}
         atts = {}
+        enhanceds = {}
+
+        def interleave_on_scalar(words, rows):
+            nc.scalar.copy(
+                out=words.rearrange("p (c i) t -> p c t i", i=4),
+                in_=rows.rearrange("p t (c i) -> p c t i", i=4),
+            )
 
         def regroup_patch(b):
             grouped = stage.tile([P, N, PACK], BF16, align_bytes=64, tag="patch_grouped")
-            nc.scalar.copy(out=grouped[:], in_=x_sb[:, b].rearrange("p j n -> p n j"))
+            interleave_on_scalar(grouped[:], x_sb[:, b])
             patch_grouped[b] = grouped
 
         def quantise_patch(b):
@@ -107,30 +121,48 @@ def tile_acd_pa_t_e_kernel(
             patch_codes[b] = codes
             patch_scales[b] = scales
 
-        def open_batch(b):
-            grouped = stage.tile([P, 2, HEADS, N, PACK], BF16, align_bytes=64, tag="qk_grouped")
-            codes = stage.tile([P, 2, HEADS, N], U32, align_bytes=64, tag="qk_codes")
-            scales = stage.tile([P, 2, HEADS, N], U8, align_bytes=64, tag="qk_scales")
-            qk_grouped[b] = grouped
-            qk_codes[b] = codes
-            qk_scales[b] = scales
+        def project_pass(out, b, side, h, t, n_cols):
+            d_cols = slice(t * P, (t + 1) * P)
+            nc.tensor.matmul_mx(
+                out=out,
+                lhsT=w_words[:, side, h, d_cols].bitcast(FP8X4),
+                lhsT_scale=w_scales[:, side, h, d_cols],
+                rhs=patch_codes[b][:, n_cols].bitcast(FP8X4),
+                rhs_scale=patch_scales[b][:, n_cols],
+                start=True,
+                stop=True,
+            )
 
-        def project(b, side, h):
-            first = (side * HEADS + h) * PACK
+        def project_for_scalar(b):
+            grouped = stage.tile([P, 2, HEADS, N, PACK], BF16, align_bytes=64, tag="qk_grouped")
+            qk_grouped[b] = grouped
+            rows = stage.tile([P, PACK, N], BF16, tag="planes")
+            planes[b] = rows
+            first = bias_column(K_SIDE, 1)
+            for half in range(2):
+                acc = planes_psum.tile([P, 2, N], F32, tag="planes_acc")
+                for i in range(2):
+                    project_pass(acc[:, i, :], b, K_SIDE, 1, 2 * half + i, slice(0, N))
+                for i in range(2):
+                    t = 2 * half + i
+                    nc.scalar.activation(
+                        out=rows[:, t, :],
+                        in_=acc[:, i, :],
+                        func=ACT.Identity,
+                        bias=bias[:, first + t : first + t + 1],
+                        scale=1.0,
+                    )
+
+        def regroup_planes(b):
+            interleave_on_scalar(qk_grouped[b][:, K_SIDE, 1], planes[b][:])
+
+        def project_for_vector(b, side, h):
+            first = bias_column(side, h)
             for nt in range(N_TILES):
                 n_cols = slice(nt * P, (nt + 1) * P)
                 acc = proj_psum.tile([P, PACK, P], F32, tag="proj")
                 for t in range(PACK):
-                    d_cols = slice(t * P, (t + 1) * P)
-                    nc.tensor.matmul_mx(
-                        out=acc[:, t, :],
-                        lhsT=w_words[:, side, h, d_cols].bitcast(FP8X4),
-                        lhsT_scale=w_scales[:, side, h, d_cols],
-                        rhs=patch_codes[b][:, n_cols].bitcast(FP8X4),
-                        rhs_scale=patch_scales[b][:, n_cols],
-                        start=True,
-                        stop=True,
-                    )
+                    project_pass(acc[:, t, :], b, side, h, t, n_cols)
                 nc.vector.tensor_tensor(
                     out=qk_grouped[b][:, side, h, n_cols, :],
                     in0=acc[:].rearrange("p t n -> p n t"),
@@ -139,14 +171,17 @@ def tile_acd_pa_t_e_kernel(
                 )
 
         def quantise_side(b, side):
+            codes = stage.tile([P, HEADS, N], U32, align_bytes=64, tag="qk_codes", bufs=4)
+            scales = stage.tile([P, HEADS, N], U8, align_bytes=64, tag="qk_scales", bufs=4)
             nc.vector.quantize_mx(
-                out=qk_codes[b][:, side].rearrange("p h n -> p (h n)").bitcast(FP8X4),
-                scales=qk_scales[b][:, side].rearrange("p h n -> p (h n)"),
+                out=codes[:].rearrange("p h n -> p (h n)").bitcast(FP8X4),
+                scales=scales[:].rearrange("p h n -> p (h n)"),
                 in_=qk_grouped[b][:, side].rearrange("p h n t -> p (h n t)"),
             )
+            qk_codes[b, side] = codes
+            qk_scales[b, side] = scales
 
         def similarity(b):
-            codes, scales = qk_codes[b], qk_scales[b]
             sim_sb = results.tile([P, HEADS, N_TILES, N], F32, tag="sim_sb")
             for h in range(HEADS):
                 sim_ps = sim_psum.tile([P, N_TILES, N], F32, tag="sim")
@@ -154,10 +189,10 @@ def tile_acd_pa_t_e_kernel(
                     q_cols = slice(qt * P, (qt + 1) * P)
                     nc.tensor.matmul_mx(
                         out=sim_ps[:, qt, :],
-                        lhsT=codes[:, Q_SIDE, h, q_cols].bitcast(FP8X4),
-                        lhsT_scale=scales[:, Q_SIDE, h, q_cols],
-                        rhs=codes[:, K_SIDE, h, :].bitcast(FP8X4),
-                        rhs_scale=scales[:, K_SIDE, h, :],
+                        lhsT=qk_codes[b, Q_SIDE][:, h, q_cols].bitcast(FP8X4),
+                        lhsT_scale=qk_scales[b, Q_SIDE][:, h, q_cols],
+                        rhs=qk_codes[b, K_SIDE][:, h, :].bitcast(FP8X4),
+                        rhs_scale=qk_scales[b, K_SIDE][:, h, :],
                         start=True,
                         stop=True,
                     )
@@ -179,7 +214,7 @@ def tile_acd_pa_t_e_kernel(
                 )
 
         def gate(b):
-            att = results.tile([P, HEADS, N], F32, tag="att")
+            att = results.tile([P, HEADS, N], F32, tag="att", bufs=4)
             nc.scalar.activation(out=att[:, 0, :], in_=diffs[b][:], func=ACT.Sigmoid, scale=1.0)
             nc.scalar.activation(out=att[:, 1, :], in_=diffs[b][:], func=ACT.Sigmoid, scale=-1.0)
             nc.sync.dma_start(
@@ -188,38 +223,55 @@ def tile_acd_pa_t_e_kernel(
             )
             atts[b] = att
 
-        def enhance(b):
-            enhanced_rows = out_1[b].rearrange("(h p j) i w -> h p (j i w)", h=HEADS, j=PACK)
+        def split_rows(b):
+            vector_rows = VECTOR_ROWS_AT_END if b >= B - 2 else VECTOR_ROWS
+            return PACK - vector_rows
+
+        def enhance_on_gpsimd(b):
+            split = split_rows(b)
+            enhanced = results.tile([P, HEADS, PACK, N], F32, tag="enhanced", bufs=4)
+            enhanceds[b] = enhanced
             for h in range(HEADS):
-                engine = nc.vector if (h == 1 and b >= B - 2) else nc.gpsimd
-                enhanced = results.tile([P, PACK, N], F32, tag="enhanced", bufs=6)
-                engine.tensor_tensor(
-                    out=enhanced[:],
-                    in0=x_sb[:, b],
-                    in1=atts[b][:, h, :].unsqueeze(1).to_broadcast([P, PACK, N]),
+                nc.gpsimd.tensor_tensor(
+                    out=enhanced[:, h, :split, :],
+                    in0=x_sb[:, b, :split, :],
+                    in1=atts[b][:, h, :].unsqueeze(1).to_broadcast([P, split, N]),
                     op=ALU.mult,
                 )
-                nc.sync.dma_start(out=enhanced_rows[h], in_=enhanced[:].rearrange("p j n -> p (j n)"))
+
+        def enhance_on_vector(b):
+            split = split_rows(b)
+            nc.vector.tensor_tensor(
+                out=enhanceds[b][:, :, split:, :],
+                in0=x_sb[:, b, split:, :].unsqueeze(1).to_broadcast([P, HEADS, PACK - split, N]),
+                in1=atts[b][:].unsqueeze(2).to_broadcast([P, HEADS, PACK - split, N]),
+                op=ALU.mult,
+            )
+            nc.sync.dma_start(
+                out=out_1[b].rearrange("(h p j) i w -> p h (j i w)", h=HEADS, j=PACK),
+                in_=enhanceds[b][:].rearrange("p h j n -> p h (j n)"),
+            )
 
         for b in range(2):
             regroup_patch(b)
             quantise_patch(b)
-        for b in range(B + 1):
+        project_for_scalar(0)
+        for b in range(B + 2):
             if b < B:
-                open_batch(b)
-                project(b, Q_SIDE, 0)
-                project(b, Q_SIDE, 1)
-            if b >= 1:
+                project_for_vector(b, Q_SIDE, 0)
+            if 1 <= b <= B:
                 similarity(b - 1)
+            if b < B:
+                regroup_planes(b)
+                project_for_vector(b, Q_SIDE, 1)
             if b + 2 < B:
                 regroup_patch(b + 2)
+            if b + 1 < B:
+                project_for_scalar(b + 1)
             if b < B:
-                project(b, K_SIDE, 0)
-            if b >= 1:
+                project_for_vector(b, K_SIDE, 0)
+            if 1 <= b <= B:
                 sum_queries(b - 1, 0)
-            if b < B:
-                project(b, K_SIDE, 1)
-            if b >= 1:
                 sum_queries(b - 1, 1)
                 gate(b - 1)
             if b < B:
@@ -228,5 +280,7 @@ def tile_acd_pa_t_e_kernel(
                 quantise_patch(b + 2)
             if b < B:
                 quantise_side(b, K_SIDE)
-            if b >= 1:
-                enhance(b - 1)
+            if 1 <= b <= B:
+                enhance_on_gpsimd(b - 1)
+            if b >= 2:
+                enhance_on_vector(b - 2)

@@ -62,21 +62,21 @@ def tile_acd_pa_t_e_kernel(
             nc.sync.dma_start(out=x_sb[:, b], in_=x[b].rearrange("(p j) i w -> p j (i w)", j=PACK))
 
         def load_weight(side, words, scales):
-            nc.sync.dma_start(
-                out=w_words[:, side].bitcast(I32),
-                in_=words.rearrange("g p d t -> p g (d t)").bitcast(I32),
-            )
             for quad in range(4):
                 nc.sync.dma_start(
                     out=w_scales[32 * quad : 32 * quad + 4, side].bitcast(I32),
                     in_=scales[:, 4 * quad : 4 * quad + 4, :].rearrange("g r d -> r g d").bitcast(I32),
                 )
+            nc.sync.dma_start(
+                out=w_words[:, side].bitcast(I32),
+                in_=words.rearrange("g p d t -> p g (d t)").bitcast(I32),
+            )
 
         load_x(0)
         nc.sync.dma_start(out=bias_rows[0:8, :], in_=q_b.rearrange("h (t p) -> (h t) p", p=P))
         nc.sync.dma_start(out=bias_rows[8:16, :], in_=k_b.rearrange("h (t p) -> (h t) p", p=P))
-        load_weight(K_SIDE, k_w_words, k_w_scales)
         load_weight(Q_SIDE, q_w_words, q_w_scales)
+        load_weight(K_SIDE, k_w_words, k_w_scales)
         for b in range(1, B):
             load_x(b)
 
@@ -133,16 +133,18 @@ def tile_acd_pa_t_e_kernel(
                 stop=True,
             )
 
-        def project_for_scalar(b):
+        def open_batch(b):
             grouped = stage.tile([P, 2, HEADS, N, PACK], BF16, align_bytes=64, tag="qk_grouped")
             qk_grouped[b] = grouped
+
+        def project_for_scalar(b):
             rows = stage.tile([P, PACK, N], BF16, tag="planes")
             planes[b] = rows
-            first = bias_column(K_SIDE, 1)
+            first = bias_column(Q_SIDE, 1)
             for half in range(2):
                 acc = planes_psum.tile([P, 2, N], F32, tag="planes_acc")
                 for i in range(2):
-                    project_pass(acc[:, i, :], b, K_SIDE, 1, 2 * half + i, slice(0, N))
+                    project_pass(acc[:, i, :], b, Q_SIDE, 1, 2 * half + i, slice(0, N))
                 for i in range(2):
                     t = 2 * half + i
                     nc.scalar.activation(
@@ -154,7 +156,7 @@ def tile_acd_pa_t_e_kernel(
                     )
 
         def regroup_planes(b):
-            interleave_on_scalar(qk_grouped[b][:, K_SIDE, 1], planes[b][:])
+            interleave_on_scalar(qk_grouped[b][:, Q_SIDE, 1], planes[b][:])
 
         def project_for_vector(b, side, h):
             first = bias_column(side, h)
@@ -255,21 +257,24 @@ def tile_acd_pa_t_e_kernel(
         for b in range(2):
             regroup_patch(b)
             quantise_patch(b)
-        project_for_scalar(0)
+        open_batch(0)
         for b in range(B + 2):
             if b < B:
                 project_for_vector(b, Q_SIDE, 0)
+            if b == 0:
+                project_for_scalar(0)
             if 1 <= b <= B:
                 similarity(b - 1)
             if b < B:
                 regroup_planes(b)
-                project_for_vector(b, Q_SIDE, 1)
+                project_for_vector(b, K_SIDE, 0)
             if b + 2 < B:
                 regroup_patch(b + 2)
             if b + 1 < B:
+                open_batch(b + 1)
                 project_for_scalar(b + 1)
             if b < B:
-                project_for_vector(b, K_SIDE, 0)
+                project_for_vector(b, K_SIDE, 1)
             if 1 <= b <= B:
                 sum_queries(b - 1, 0)
                 sum_queries(b - 1, 1)

@@ -23,8 +23,9 @@ HD = 512
 N_TILES = N // P
 Q_SIDE, K_SIDE = 0, 1
 INV_SQRT_HD = 1.0 / math.sqrt(HD)
+LAST = B - 1
 VECTOR_ROWS = 1
-VECTOR_ROWS_AT_END = 3
+VECTOR_ROWS_OF = {LAST - 1: 2, LAST: 4}
 
 FLOPS = 2 * B * HEADS * N * C * HD * 2 + 2 * B * HEADS * N * N * HD
 
@@ -57,6 +58,8 @@ def tile_acd_pa_t_e_kernel(
         nc.vector.memset(plus_ones[:], 1.0)
         nc.vector.memset(minus_ones[:], -1.0)
         make_identity(nc, identity[:])
+        warm = keep.tile([P, 1], F32)
+        nc.scalar.activation(out=warm[:], in_=plus_ones[:, 0:1], func=ACT.Sigmoid, scale=1.0)
 
         def load_x(b):
             nc.sync.dma_start(out=x_sb[:, b], in_=x[b].rearrange("(p j) i w -> p j (i w)", j=PACK))
@@ -110,6 +113,15 @@ def tile_acd_pa_t_e_kernel(
             interleave_on_scalar(grouped[:], x_sb[:, b])
             patch_grouped[b] = grouped
 
+        def regroup_patch_halves(b):
+            grouped = stage.tile([P, N, PACK], BF16, align_bytes=64, tag="patch_grouped")
+            interleave_on_scalar(grouped[:, :P, :], x_sb[:, b, :, :P])
+            nc.vector.tensor_copy(
+                out=grouped[:, P:, :].rearrange("p (c i) t -> p c t i", i=4),
+                in_=x_sb[:, b, :, P:].rearrange("p t (c i) -> p c t i", i=4),
+            )
+            patch_grouped[b] = grouped
+
         def quantise_patch(b):
             codes = stage.tile([P, N], U32, align_bytes=64, tag="patch_codes", bufs=3)
             scales = stage.tile([P, N], U8, align_bytes=64, tag="patch_scales", bufs=3)
@@ -158,9 +170,26 @@ def tile_acd_pa_t_e_kernel(
         def regroup_planes(b):
             interleave_on_scalar(qk_grouped[b][:, Q_SIDE, 1], planes[b][:])
 
-        def project_for_vector(b, side, h):
+        def project_half_for_scalar(b, side, h, nt):
+            rows = stage.tile([P, PACK, P], BF16, tag="half_planes", bufs=1)
             first = bias_column(side, h)
-            for nt in range(N_TILES):
+            n_cols = slice(nt * P, (nt + 1) * P)
+            acc = planes_psum.tile([P, PACK, P], F32, tag="planes_acc")
+            for t in range(PACK):
+                project_pass(acc[:, t, :], b, side, h, t, n_cols)
+            for t in range(PACK):
+                nc.scalar.activation(
+                    out=rows[:, t, :],
+                    in_=acc[:, t, :],
+                    func=ACT.Identity,
+                    bias=bias[:, first + t : first + t + 1],
+                    scale=1.0,
+                )
+            interleave_on_scalar(qk_grouped[b][:, side, h, n_cols, :], rows[:])
+
+        def project_for_vector(b, side, h, tiles=range(N_TILES)):
+            first = bias_column(side, h)
+            for nt in tiles:
                 n_cols = slice(nt * P, (nt + 1) * P)
                 acc = proj_psum.tile([P, PACK, P], F32, tag="proj")
                 for t in range(PACK):
@@ -172,16 +201,28 @@ def tile_acd_pa_t_e_kernel(
                     op=ALU.add,
                 )
 
-        def quantise_side(b, side):
+        def open_codes(b, side):
             codes = stage.tile([P, HEADS, N], U32, align_bytes=64, tag="qk_codes", bufs=4)
             scales = stage.tile([P, HEADS, N], U8, align_bytes=64, tag="qk_scales", bufs=4)
+            qk_codes[b, side] = codes
+            qk_scales[b, side] = scales
+
+        def quantise_head(b, side, h):
+            nc.vector.quantize_mx(
+                out=qk_codes[b, side][:, h, :].bitcast(FP8X4),
+                scales=qk_scales[b, side][:, h, :],
+                in_=qk_grouped[b][:, side, h].rearrange("p n t -> p (n t)"),
+            )
+
+        def quantise_side(b, side):
+            open_codes(b, side)
+            codes = qk_codes[b, side]
+            scales = qk_scales[b, side]
             nc.vector.quantize_mx(
                 out=codes[:].rearrange("p h n -> p (h n)").bitcast(FP8X4),
                 scales=scales[:].rearrange("p h n -> p (h n)"),
                 in_=qk_grouped[b][:, side].rearrange("p h n t -> p (h n t)"),
             )
-            qk_codes[b, side] = codes
-            qk_scales[b, side] = scales
 
         def similarity(b):
             sim_sb = results.tile([P, HEADS, N_TILES, N], F32, tag="sim_sb")
@@ -198,7 +239,14 @@ def tile_acd_pa_t_e_kernel(
                         start=True,
                         stop=True,
                     )
-                nc.scalar.activation(out=sim_sb[:, h], in_=sim_ps[:], func=ACT.Copy, scale=INV_SQRT_HD)
+                if b == LAST and h == 1:
+                    nc.vector.tensor_scalar(
+                        out=sim_sb[:, h], in0=sim_ps[:], scalar1=INV_SQRT_HD, scalar2=None, op0=ALU.mult
+                    )
+                else:
+                    nc.scalar.activation(
+                        out=sim_sb[:, h], in_=sim_ps[:], func=ACT.Copy, scale=INV_SQRT_HD
+                    )
             nc.sync.dma_start(out=out_2[b].rearrange("h (qt p) k -> p h qt k", p=P), in_=sim_sb[:])
             sim_sbs[b] = sim_sb
 
@@ -226,8 +274,7 @@ def tile_acd_pa_t_e_kernel(
             atts[b] = att
 
         def split_rows(b):
-            vector_rows = VECTOR_ROWS_AT_END if b >= B - 2 else VECTOR_ROWS
-            return PACK - vector_rows
+            return PACK - VECTOR_ROWS_OF.get(b, VECTOR_ROWS)
 
         def enhance_on_gpsimd(b):
             split = split_rows(b)
@@ -254,38 +301,69 @@ def tile_acd_pa_t_e_kernel(
                 in_=enhanceds[b][:].rearrange("p h j n -> p h (j n)"),
             )
 
-        for b in range(2):
-            regroup_patch(b)
-            quantise_patch(b)
+        def enhance_last():
+            enhanced = results.tile([P, HEADS, PACK, N], F32, tag="enhanced", bufs=4)
+            rows = out_1[LAST].rearrange("(h p j) i w -> p h (j i w)", h=HEADS, j=PACK)
+            for h in range(HEADS):
+                nc.vector.tensor_tensor(
+                    out=enhanced[:, h],
+                    in0=x_sb[:, LAST],
+                    in1=atts[LAST][:, h, :].unsqueeze(1).to_broadcast([P, PACK, N]),
+                    op=ALU.mult,
+                )
+                nc.sync.dma_start(out=rows[:, h], in_=enhanced[:, h].rearrange("p j n -> p (j n)"))
+
+        regroup_patch_halves(0)
+        quantise_patch(0)
         open_batch(0)
-        for b in range(B + 2):
-            if b < B:
-                project_for_vector(b, Q_SIDE, 0)
+        for b in range(LAST):
+            project_for_vector(b, Q_SIDE, 0)
             if b == 0:
                 project_for_scalar(0)
-            if 1 <= b <= B:
+            else:
                 similarity(b - 1)
-            if b < B:
-                regroup_planes(b)
-                project_for_vector(b, K_SIDE, 0)
+            regroup_planes(b)
+            project_for_vector(b, K_SIDE, 0)
+            if b == 0:
+                regroup_patch(1)
             if b + 2 < B:
                 regroup_patch(b + 2)
-            if b + 1 < B:
-                open_batch(b + 1)
+            open_batch(b + 1)
+            if b > 0:
                 project_for_scalar(b + 1)
-            if b < B:
-                project_for_vector(b, K_SIDE, 1)
-            if 1 <= b <= B:
+            project_for_vector(b, K_SIDE, 1)
+            if b == 0:
+                quantise_patch(1)
+                project_for_scalar(1)
+            else:
                 sum_queries(b - 1, 0)
                 sum_queries(b - 1, 1)
                 gate(b - 1)
-            if b < B:
-                quantise_side(b, Q_SIDE)
+            quantise_side(b, Q_SIDE)
             if b + 2 < B:
                 quantise_patch(b + 2)
-            if b < B:
-                quantise_side(b, K_SIDE)
-            if 1 <= b <= B:
+            quantise_side(b, K_SIDE)
+            if b >= 1:
                 enhance_on_gpsimd(b - 1)
             if b >= 2:
                 enhance_on_vector(b - 2)
+
+        project_for_vector(LAST, Q_SIDE, 0)
+        similarity(LAST - 1)
+        regroup_planes(LAST)
+        project_for_vector(LAST, K_SIDE, 0)
+        project_half_for_scalar(LAST, K_SIDE, 1, 1)
+        project_for_vector(LAST, K_SIDE, 1, tiles=[0])
+        sum_queries(LAST - 1, 0)
+        sum_queries(LAST - 1, 1)
+        gate(LAST - 1)
+        quantise_side(LAST, Q_SIDE)
+        quantise_side(LAST, K_SIDE)
+        enhance_on_gpsimd(LAST - 1)
+        enhance_on_vector(LAST - 2)
+        similarity(LAST)
+        sum_queries(LAST, 0)
+        sum_queries(LAST, 1)
+        gate(LAST)
+        enhance_on_vector(LAST - 1)
+        enhance_last()

@@ -25,7 +25,9 @@ Q_SIDE, K_SIDE = 0, 1
 INV_SQRT_HD = 1.0 / math.sqrt(HD)
 LAST = B - 1
 VECTOR_ROWS = 1
-VECTOR_ROWS_OF = {LAST - 1: 2, LAST: 4}
+VECTOR_ROWS_OF = {}
+LATE = [LAST - 2]
+HALF = [0, 15]
 
 FLOPS = 2 * B * HEADS * N * C * HD * 2 + 2 * B * HEADS * N * N * HD
 
@@ -52,6 +54,7 @@ def tile_acd_pa_t_e_kernel(
         bias = keep.tile([P, 2 * HEADS * PACK], F32)
         plus_ones = keep.tile([P, P], F32)
         minus_ones = keep.tile([P, P], F32)
+        minus_bias = keep.tile([P, PACK], F32)
 
         nc.vector.memset(w_scales[:].rearrange("p s h d -> p (s h d)").bitcast(I32), 0)
         nc.vector.memset(bias_rows[:], 0.0)
@@ -79,8 +82,9 @@ def tile_acd_pa_t_e_kernel(
         nc.sync.dma_start(out=bias_rows[0:8, :], in_=q_b.rearrange("h (t p) -> (h t) p", p=P))
         nc.sync.dma_start(out=bias_rows[8:16, :], in_=k_b.rearrange("h (t p) -> (h t) p", p=P))
         load_weight(Q_SIDE, q_w_words, q_w_scales)
+        load_x(1)
         load_weight(K_SIDE, k_w_words, k_w_scales)
-        for b in range(1, B):
+        for b in range(2, B):
             load_x(b)
 
         bias_ps = gate_psum.tile([P, P], BF16, tag="gate")
@@ -90,14 +94,25 @@ def tile_acd_pa_t_e_kernel(
         def bias_column(side, h):
             return (side * HEADS + h) * PACK
 
+        first_q1 = bias_column(Q_SIDE, 1)
+        nc.vector.tensor_scalar(
+            out=minus_bias[:], in0=bias[:, first_q1 : first_q1 + PACK], scalar1=-1.0, scalar2=None, op0=ALU.mult
+        )
+
         patch_grouped = {}
         patch_codes = {}
         patch_scales = {}
         planes = {}
+        half_planes = {}
+
+        def vector_tiles(b):
+            return [0] if b in HALF else [0, 1]
+
         qk_grouped = {}
         qk_codes = {}
         qk_scales = {}
         sim_sbs = {}
+        folds = {}
         diffs = {}
         atts = {}
         enhanceds = {}
@@ -152,7 +167,6 @@ def tile_acd_pa_t_e_kernel(
         def project_for_scalar(b):
             rows = stage.tile([P, PACK, N], BF16, tag="planes")
             planes[b] = rows
-            first = bias_column(Q_SIDE, 1)
             for half in range(2):
                 acc = planes_psum.tile([P, 2, N], F32, tag="planes_acc")
                 for i in range(2):
@@ -163,15 +177,19 @@ def tile_acd_pa_t_e_kernel(
                         out=rows[:, t, :],
                         in_=acc[:, i, :],
                         func=ACT.Identity,
-                        bias=bias[:, first + t : first + t + 1],
-                        scale=1.0,
+                        bias=minus_bias[:, t : t + 1],
+                        scale=-1.0,
                     )
 
         def regroup_planes(b):
-            interleave_on_scalar(qk_grouped[b][:, Q_SIDE, 1], planes[b][:])
+            if b > 0:
+                interleave_on_scalar(qk_grouped[b][:, Q_SIDE, 1], planes[b][:])
+            if b in HALF:
+                interleave_on_scalar(qk_grouped[b][:, K_SIDE, 1, P:, :], half_planes[b][:])
 
         def project_half_for_scalar(b, side, h, nt):
-            rows = stage.tile([P, PACK, P], BF16, tag="half_planes", bufs=1)
+            rows = stage.tile([P, PACK, P], BF16, tag="half_planes")
+            half_planes[b] = rows
             first = bias_column(side, h)
             n_cols = slice(nt * P, (nt + 1) * P)
             acc = planes_psum.tile([P, PACK, P], F32, tag="planes_acc")
@@ -185,7 +203,6 @@ def tile_acd_pa_t_e_kernel(
                     bias=bias[:, first + t : first + t + 1],
                     scale=1.0,
                 )
-            interleave_on_scalar(qk_grouped[b][:, side, h, n_cols, :], rows[:])
 
         def project_for_vector(b, side, h, tiles=range(N_TILES)):
             first = bias_column(side, h)
@@ -194,12 +211,15 @@ def tile_acd_pa_t_e_kernel(
                 acc = proj_psum.tile([P, PACK, P], F32, tag="proj")
                 for t in range(PACK):
                     project_pass(acc[:, t, :], b, side, h, t, n_cols)
-                nc.vector.tensor_tensor(
-                    out=qk_grouped[b][:, side, h, n_cols, :],
-                    in0=acc[:].rearrange("p t n -> p n t"),
-                    in1=bias[:, first : first + PACK].unsqueeze(1).to_broadcast([P, P, PACK]),
-                    op=ALU.add,
-                )
+                words = qk_grouped[b][:, side, h, n_cols, :]
+                rows = acc[:].rearrange("p t n -> p n t")
+                bias_words = bias[:, first : first + PACK].unsqueeze(1).to_broadcast([P, P, PACK])
+                if (side, h) == (Q_SIDE, 1):
+                    nc.vector.scalar_tensor_tensor(
+                        out=words, in0=rows, scalar=-1.0, in1=bias_words, op0=ALU.mult, op1=ALU.subtract
+                    )
+                else:
+                    nc.vector.tensor_tensor(out=words, in0=rows, in1=bias_words, op=ALU.add)
 
         def open_codes(b, side):
             codes = stage.tile([P, HEADS, N], U32, align_bytes=64, tag="qk_codes", bufs=4)
@@ -224,31 +244,51 @@ def tile_acd_pa_t_e_kernel(
                 in_=qk_grouped[b][:, side].rearrange("p h n t -> p (h n t)"),
             )
 
+        def similarity_pass(out, b, h, qt, start, stop):
+            q_cols = slice(qt * P, (qt + 1) * P)
+            nc.tensor.matmul_mx(
+                out=out,
+                lhsT=qk_codes[b, Q_SIDE][:, h, q_cols].bitcast(FP8X4),
+                lhsT_scale=qk_scales[b, Q_SIDE][:, h, q_cols],
+                rhs=qk_codes[b, K_SIDE][:, h, :].bitcast(FP8X4),
+                rhs_scale=qk_scales[b, K_SIDE][:, h, :],
+                start=start,
+                stop=stop,
+            )
+
+        def fold(b):
+            folded_ps = proj_psum.tile([P, PACK, P], F32, tag="proj")
+            out = folded_ps[:].rearrange("p t n -> p (t n)")[:, :N]
+            for h in range(HEADS):
+                for qt in range(N_TILES):
+                    similarity_pass(
+                        out, b, h, qt,
+                        start=(h == 0 and qt == 0),
+                        stop=(h == HEADS - 1 and qt == N_TILES - 1),
+                    )
+            folded = results.tile([P, N], F32, tag="folded", bufs=2)
+            nc.scalar.activation(out=folded[:], in_=out, func=ACT.Copy, scale=INV_SQRT_HD)
+            folds[b] = folded
+
+        def sum_fold(b):
+            diff = gate_psum.tile([P, N], F32, tag="gate")
+            diffs[b] = diff
+            nc.tensor.matmul(out=diff[:], lhsT=plus_ones[:], rhs=folds[b][:], start=True, stop=True)
+
         def similarity(b):
             sim_sb = results.tile([P, HEADS, N_TILES, N], F32, tag="sim_sb")
             for h in range(HEADS):
+                scale = INV_SQRT_HD if h == 0 else -INV_SQRT_HD
                 sim_ps = sim_psum.tile([P, N_TILES, N], F32, tag="sim")
                 for qt in range(N_TILES):
-                    q_cols = slice(qt * P, (qt + 1) * P)
-                    nc.tensor.matmul_mx(
-                        out=sim_ps[:, qt, :],
-                        lhsT=qk_codes[b, Q_SIDE][:, h, q_cols].bitcast(FP8X4),
-                        lhsT_scale=qk_scales[b, Q_SIDE][:, h, q_cols],
-                        rhs=qk_codes[b, K_SIDE][:, h, :].bitcast(FP8X4),
-                        rhs_scale=qk_scales[b, K_SIDE][:, h, :],
-                        start=True,
-                        stop=True,
-                    )
-                if b == LAST and h == 1:
-                    nc.vector.tensor_scalar(
-                        out=sim_sb[:, h], in0=sim_ps[:], scalar1=INV_SQRT_HD, scalar2=None, op0=ALU.mult
-                    )
-                else:
-                    nc.scalar.activation(
-                        out=sim_sb[:, h], in_=sim_ps[:], func=ACT.Copy, scale=INV_SQRT_HD
-                    )
-            nc.sync.dma_start(out=out_2[b].rearrange("h (qt p) k -> p h qt k", p=P), in_=sim_sb[:])
+                    similarity_pass(sim_ps[:, qt, :], b, h, qt, start=True, stop=True)
+                nc.scalar.activation(out=sim_sb[:, h], in_=sim_ps[:], func=ACT.Copy, scale=scale)
             sim_sbs[b] = sim_sb
+            if b < LAST:
+                store_similarity(b)
+
+        def store_similarity(b):
+            nc.sync.dma_start(out=out_2[b].rearrange("h (qt p) k -> p h qt k", p=P), in_=sim_sbs[b][:])
 
         def sum_queries(b, h):
             if h == 0:
@@ -267,18 +307,22 @@ def tile_acd_pa_t_e_kernel(
             att = results.tile([P, HEADS, N], F32, tag="att", bufs=4)
             nc.scalar.activation(out=att[:, 0, :], in_=diffs[b][:], func=ACT.Sigmoid, scale=1.0)
             nc.scalar.activation(out=att[:, 1, :], in_=diffs[b][:], func=ACT.Sigmoid, scale=-1.0)
+            atts[b] = att
+            if b < LAST:
+                store_gate(b)
+
+        def store_gate(b):
             nc.sync.dma_start(
                 out=out_0[b : b + 1].rearrange("o h i w -> o (h i w)"),
-                in_=att[0:1].rearrange("o h n -> o (h n)"),
+                in_=atts[b][0:1].rearrange("o h n -> o (h n)"),
             )
-            atts[b] = att
 
         def split_rows(b):
             return PACK - VECTOR_ROWS_OF.get(b, VECTOR_ROWS)
 
         def enhance_on_gpsimd(b):
             split = split_rows(b)
-            enhanced = results.tile([P, HEADS, PACK, N], F32, tag="enhanced", bufs=4)
+            enhanced = results.tile([P, HEADS, PACK, N], F32, tag="enhanced", bufs=6)
             enhanceds[b] = enhanced
             for h in range(HEADS):
                 nc.gpsimd.tensor_tensor(
@@ -288,6 +332,12 @@ def tile_acd_pa_t_e_kernel(
                     op=ALU.mult,
                 )
 
+        def store_rows(b, first, end):
+            nc.sync.dma_start(
+                out=out_1[b].rearrange("(h p j) i w -> p h j (i w)", h=HEADS, j=PACK)[:, :, first:end, :],
+                in_=enhanceds[b][:, :, first:end, :],
+            )
+
         def enhance_on_vector(b):
             split = split_rows(b)
             nc.vector.tensor_tensor(
@@ -296,74 +346,78 @@ def tile_acd_pa_t_e_kernel(
                 in1=atts[b][:].unsqueeze(2).to_broadcast([P, HEADS, PACK - split, N]),
                 op=ALU.mult,
             )
-            nc.sync.dma_start(
-                out=out_1[b].rearrange("(h p j) i w -> p h (j i w)", h=HEADS, j=PACK),
-                in_=enhanceds[b][:].rearrange("p h j n -> p h (j n)"),
-            )
+            store_rows(b, split if b in LATE else 0, PACK)
 
-        def enhance_last():
-            enhanced = results.tile([P, HEADS, PACK, N], F32, tag="enhanced", bufs=4)
-            rows = out_1[LAST].rearrange("(h p j) i w -> p h (j i w)", h=HEADS, j=PACK)
+        def enhance_by_heads(b):
+            enhanced = results.tile([P, HEADS, PACK, N], F32, tag="enhanced", bufs=6)
+            rows = out_1[b].rearrange("(h p j) i w -> p h j (i w)", h=HEADS, j=PACK)
             for h in range(HEADS):
-                nc.vector.tensor_tensor(
-                    out=enhanced[:, h],
-                    in0=x_sb[:, LAST],
-                    in1=atts[LAST][:, h, :].unsqueeze(1).to_broadcast([P, PACK, N]),
-                    op=ALU.mult,
-                )
-                nc.sync.dma_start(out=rows[:, h], in_=enhanced[:, h].rearrange("p j n -> p (j n)"))
+                parts = [slice(0, 2), slice(2, 4)] if (b, h) == (LAST, 1) else [slice(0, 4)]
+                for j in parts:
+                    nc.vector.tensor_tensor(
+                        out=enhanced[:, h, j],
+                        in0=x_sb[:, b, j],
+                        in1=atts[b][:, h, :].unsqueeze(1).to_broadcast([P, j.stop - j.start, N]),
+                        op=ALU.mult,
+                    )
+                    nc.sync.dma_start(out=rows[:, h, j], in_=enhanced[:, h, j])
 
         regroup_patch_halves(0)
         quantise_patch(0)
         open_batch(0)
+        regroup_patch(1)
         for b in range(LAST):
             project_for_vector(b, Q_SIDE, 0)
             if b == 0:
-                project_for_scalar(0)
-            else:
+                project_for_vector(0, Q_SIDE, 1)
+            if b > 0:
                 similarity(b - 1)
-            regroup_planes(b)
+                regroup_planes(b)
             project_for_vector(b, K_SIDE, 0)
-            if b == 0:
-                regroup_patch(1)
             if b + 2 < B:
                 regroup_patch(b + 2)
             open_batch(b + 1)
             if b > 0:
                 project_for_scalar(b + 1)
-            project_for_vector(b, K_SIDE, 1)
+            project_for_vector(b, K_SIDE, 1, tiles=vector_tiles(b))
             if b == 0:
+                if 0 in HALF:
+                    project_half_for_scalar(0, K_SIDE, 1, 1)
+                    regroup_planes(0)
                 quantise_patch(1)
                 project_for_scalar(1)
-            else:
+            if b > 0:
                 sum_queries(b - 1, 0)
                 sum_queries(b - 1, 1)
                 gate(b - 1)
+            if b + 1 in HALF:
+                project_half_for_scalar(b + 1, K_SIDE, 1, 1)
             quantise_side(b, Q_SIDE)
-            if b + 2 < B:
-                quantise_patch(b + 2)
             quantise_side(b, K_SIDE)
             if b >= 1:
                 enhance_on_gpsimd(b - 1)
-            if b >= 2:
+            if b >= 2 and b - 2 not in LATE:
                 enhance_on_vector(b - 2)
+            if b + 2 < B:
+                quantise_patch(b + 2)
 
         project_for_vector(LAST, Q_SIDE, 0)
+        fold(LAST - 1)
         similarity(LAST - 1)
         regroup_planes(LAST)
         project_for_vector(LAST, K_SIDE, 0)
-        project_half_for_scalar(LAST, K_SIDE, 1, 1)
-        project_for_vector(LAST, K_SIDE, 1, tiles=[0])
-        sum_queries(LAST - 1, 0)
-        sum_queries(LAST - 1, 1)
+        project_for_vector(LAST, K_SIDE, 1, tiles=vector_tiles(LAST))
+        store_rows(LAST - 2, 0, split_rows(LAST - 2))
+        sum_fold(LAST - 1)
         gate(LAST - 1)
         quantise_side(LAST, Q_SIDE)
-        quantise_side(LAST, K_SIDE)
-        enhance_on_gpsimd(LAST - 1)
         enhance_on_vector(LAST - 2)
+        quantise_side(LAST, K_SIDE)
+        fold(LAST)
         similarity(LAST)
-        sum_queries(LAST, 0)
-        sum_queries(LAST, 1)
+        sum_fold(LAST)
         gate(LAST)
-        enhance_on_vector(LAST - 1)
-        enhance_last()
+        enhance_by_heads(LAST - 1)
+        store_similarity(LAST)
+        store_gate(LAST)
+        enhance_by_heads(LAST)

@@ -67,37 +67,47 @@ def tile_acd_pa_t_e_kernel(
         def load_x(b):
             nc.sync.dma_start(out=x_sb[:, b], in_=x[b].rearrange("(p j) i w -> p j (i w)", j=PACK))
 
-        def load_weight(side, words, scales):
+        def load_words(side, h, words):
+            nc.sync.dma_start(
+                out=w_words[:, side, h].bitcast(I32),
+                in_=words[h].rearrange("p d t -> p (d t)").bitcast(I32),
+            )
+
+        def load_scales(side, scales):
             for quad in range(4):
                 nc.sync.dma_start(
                     out=w_scales[32 * quad : 32 * quad + 4, side].bitcast(I32),
                     in_=scales[:, 4 * quad : 4 * quad + 4, :].rearrange("g r d -> r g d").bitcast(I32),
                 )
-            nc.sync.dma_start(
-                out=w_words[:, side].bitcast(I32),
-                in_=words.rearrange("g p d t -> p g (d t)").bitcast(I32),
-            )
 
         load_x(0)
+        load_scales(Q_SIDE, q_w_scales)
         nc.sync.dma_start(out=bias_rows[0:8, :], in_=q_b.rearrange("h (t p) -> (h t) p", p=P))
         nc.sync.dma_start(out=bias_rows[8:16, :], in_=k_b.rearrange("h (t p) -> (h t) p", p=P))
-        load_weight(Q_SIDE, q_w_words, q_w_scales)
+        load_words(Q_SIDE, 0, q_w_words)
+        load_words(Q_SIDE, 1, q_w_words)
         load_x(1)
-        load_weight(K_SIDE, k_w_words, k_w_scales)
+        load_scales(K_SIDE, k_w_scales)
+        load_words(K_SIDE, 0, k_w_words)
+        load_words(K_SIDE, 1, k_w_words)
         for b in range(2, B):
             load_x(b)
 
-        bias_ps = gate_psum.tile([P, P], BF16, tag="gate")
-        nc.tensor.transpose(bias_ps[:], bias_rows[:], identity[:])
-        nc.vector.tensor_copy(out=bias[:], in_=bias_ps[:, 0 : 2 * HEADS * PACK])
 
         def bias_column(side, h):
             return (side * HEADS + h) * PACK
 
-        first_q1 = bias_column(Q_SIDE, 1)
-        nc.vector.tensor_scalar(
-            out=minus_bias[:], in0=bias[:, first_q1 : first_q1 + PACK], scalar1=-1.0, scalar2=None, op0=ALU.mult
-        )
+
+        def prepare_bias():
+            bias_ps = gate_psum.tile([P, P], BF16, tag="gate")
+            nc.tensor.transpose(bias_ps[:], bias_rows[:], identity[:])
+            nc.vector.tensor_copy(out=bias[:], in_=bias_ps[:, 0 : 2 * HEADS * PACK])
+
+        def negate_bias():
+            first_q1 = bias_column(Q_SIDE, 1)
+            nc.vector.tensor_scalar(
+                out=minus_bias[:], in0=bias[:, first_q1 : first_q1 + PACK], scalar1=-1.0, scalar2=None, op0=ALU.mult
+            )
 
         patch_grouped = {}
         patch_codes = {}
@@ -184,8 +194,9 @@ def tile_acd_pa_t_e_kernel(
         def regroup_planes(b):
             if b > 0:
                 interleave_on_scalar(qk_grouped[b][:, Q_SIDE, 1], planes[b][:])
-            if b in HALF:
-                interleave_on_scalar(qk_grouped[b][:, K_SIDE, 1, P:, :], half_planes[b][:])
+
+        def regroup_half(b):
+            interleave_on_scalar(qk_grouped[b][:, K_SIDE, 1, P:, :], half_planes[b][:])
 
         def project_half_for_scalar(b, side, h, nt):
             rows = stage.tile([P, PACK, P], BF16, tag="half_planes")
@@ -257,8 +268,8 @@ def tile_acd_pa_t_e_kernel(
             )
 
         def fold(b):
-            folded_ps = proj_psum.tile([P, PACK, P], F32, tag="proj")
-            out = folded_ps[:].rearrange("p t n -> p (t n)")[:, :N]
+            folded_ps = planes_psum.tile([P, 2, N], F32, tag="planes_acc")
+            out = folded_ps[:, 0, :]
             for h in range(HEADS):
                 for qt in range(N_TILES):
                     similarity_pass(
@@ -308,8 +319,6 @@ def tile_acd_pa_t_e_kernel(
             nc.scalar.activation(out=att[:, 0, :], in_=diffs[b][:], func=ACT.Sigmoid, scale=1.0)
             nc.scalar.activation(out=att[:, 1, :], in_=diffs[b][:], func=ACT.Sigmoid, scale=-1.0)
             atts[b] = att
-            if b < LAST:
-                store_gate(b)
 
         def store_gate(b):
             nc.sync.dma_start(
@@ -338,6 +347,12 @@ def tile_acd_pa_t_e_kernel(
                 in_=enhanceds[b][:, :, first:end, :],
             )
 
+        def store_gpsimd_rows(b, h):
+            nc.sync.dma_start(
+                out=out_1[b].rearrange("(h p j) i w -> p h j (i w)", h=HEADS, j=PACK)[:, h, : split_rows(b), :],
+                in_=enhanceds[b][:, h, : split_rows(b), :],
+            )
+
         def enhance_on_vector(b):
             split = split_rows(b)
             nc.vector.tensor_tensor(
@@ -362,8 +377,17 @@ def tile_acd_pa_t_e_kernel(
                     )
                     nc.sync.dma_start(out=rows[:, h, j], in_=enhanced[:, h, j])
 
+        def keep_tensor_warm(passes, rhs):
+            idle = planes_psum.tile([P, 2 * N], F32, tag="planes_acc")
+            for i in range(passes):
+                nc.tensor.matmul(
+                    out=idle[:, : rhs.shape[1]], lhsT=identity[:], rhs=rhs, start=True, stop=True
+                )
+
         regroup_patch_halves(0)
         quantise_patch(0)
+        keep_tensor_warm(24, identity[:])
+        prepare_bias()
         open_batch(0)
         regroup_patch(1)
         for b in range(LAST):
@@ -374,7 +398,7 @@ def tile_acd_pa_t_e_kernel(
                 similarity(b - 1)
                 regroup_planes(b)
             project_for_vector(b, K_SIDE, 0)
-            if b + 2 < B:
+            if 1 <= b and b + 2 < B:
                 regroup_patch(b + 2)
             open_batch(b + 1)
             if b > 0:
@@ -383,8 +407,10 @@ def tile_acd_pa_t_e_kernel(
             if b == 0:
                 if 0 in HALF:
                     project_half_for_scalar(0, K_SIDE, 1, 1)
-                    regroup_planes(0)
+                    regroup_half(0)
+                regroup_patch(2)
                 quantise_patch(1)
+                negate_bias()
                 project_for_scalar(1)
             if b > 0:
                 sum_queries(b - 1, 0)
@@ -398,21 +424,28 @@ def tile_acd_pa_t_e_kernel(
                 enhance_on_gpsimd(b - 1)
             if b >= 2 and b - 2 not in LATE:
                 enhance_on_vector(b - 2)
+            if b >= 1:
+                store_gate(b - 1)
             if b + 2 < B:
                 quantise_patch(b + 2)
 
-        project_for_vector(LAST, Q_SIDE, 0)
-        fold(LAST - 1)
-        similarity(LAST - 1)
         regroup_planes(LAST)
-        project_for_vector(LAST, K_SIDE, 0)
+        project_for_vector(LAST, Q_SIDE, 0)
+        project_for_vector(LAST, K_SIDE, 0, tiles=[0])
+        fold(LAST - 1)
+        store_gpsimd_rows(LAST - 2, 0)
+        project_for_vector(LAST, K_SIDE, 0, tiles=[1])
+        similarity(LAST - 1)
+        regroup_half(LAST)
+        store_gpsimd_rows(LAST - 2, 1)
         project_for_vector(LAST, K_SIDE, 1, tiles=vector_tiles(LAST))
-        store_rows(LAST - 2, 0, split_rows(LAST - 2))
         sum_fold(LAST - 1)
+        keep_tensor_warm(4, x_sb[:, LAST, 0:2, :].rearrange("p j n -> p (j n)"))
         gate(LAST - 1)
         quantise_side(LAST, Q_SIDE)
-        enhance_on_vector(LAST - 2)
         quantise_side(LAST, K_SIDE)
+        enhance_on_vector(LAST - 2)
+        store_gate(LAST - 1)
         fold(LAST)
         similarity(LAST)
         sum_fold(LAST)

import math
from contextlib import ExitStack

import concourse.mybir as mybir
from concourse.masks import make_identity

FP8X4 = mybir.dt.float8_e4m3fn_x4
BF16 = mybir.dt.bfloat16
F32 = mybir.dt.float32
I32 = mybir.dt.int32
U32 = mybir.dt.uint32
U8 = mybir.dt.uint8
ACT = mybir.ActivationFunctionType
ALU = mybir.AluOpType

P = 128
PACK = 4
B = 16
C = 512
N = 256
HEADS = 2
HD = 512
N_TILES = N // P
Q_SIDE, K_SIDE = 0, 1
INV_SQRT_HD = 1.0 / math.sqrt(HD)
LAST = B - 1
VECTOR_ROWS = 1
VECTOR_ROWS_OF = {}
LATE = [LAST - 2]
HALF = [0, 15]

FLOPS = 2 * B * HEADS * N * C * HD * 2 + 2 * B * HEADS * N * N * HD


def tile_acd_pa_t_e_kernel(
    tc, x, q_w_words, q_w_scales, q_b, k_w_words, k_w_scales, k_b, out_0, out_1, out_2
):
    nc = tc.nc
    with ExitStack() as ctx:
        keep = ctx.enter_context(tc.tile_pool(name="keep", bufs=1))
        stage = ctx.enter_context(tc.tile_pool(name="stage", bufs=2))
        results = ctx.enter_context(tc.tile_pool(name="results", bufs=3))
        proj_psum = ctx.enter_context(tc.psum_pool(name="proj_psum", bufs=3))
        planes_psum = ctx.enter_context(tc.psum_pool(name="planes_psum", bufs=2))
        sim_psum = ctx.enter_context(tc.psum_pool(name="sim_psum", bufs=2))
        gate_psum = ctx.enter_context(tc.psum_pool(name="gate_psum", bufs=1))
        ctx.enter_context(tc.manual_schedule())

        x_sb = keep.tile([P, B, PACK, N], BF16)
        w_words = keep.tile([P, 2, HEADS, HD], U32, align_bytes=64)
        w_scales = keep.tile([P, 2, HEADS, HD], U8, align_bytes=64)
        bias_rows = keep.tile([P, P], BF16)
        identity = keep.tile([P, P], BF16)
        bias = keep.tile([P, 2 * HEADS * PACK], F32)
        plus_ones = keep.tile([P, P], F32)
        minus_ones = keep.tile([P, P], F32)
        minus_bias = keep.tile([P, PACK], F32)

        nc.vector.memset(w_scales[:].rearrange("p s h d -> p (s h d)").bitcast(I32), 0)
        nc.vector.memset(bias_rows[:], 0.0)
        nc.vector.memset(plus_ones[:], 1.0)
        nc.vector.memset(minus_ones[:], -1.0)
        make_identity(nc, identity[:])
        warm = keep.tile([P, 1], F32)
        nc.scalar.activation(out=warm[:], in_=plus_ones[:, 0:1], func=ACT.Sigmoid, scale=1.0)

        def load_x(b):
            nc.sync.dma_start(out=x_sb[:, b], in_=x[b].rearrange("(p j) i w -> p j (i w)", j=PACK))

        def load_words(side, h, words):
            nc.sync.dma_start(
                out=w_words[:, side, h].bitcast(I32),
                in_=words[h].rearrange("p d t -> p (d t)").bitcast(I32),
            )

        def load_scales(side, scales):
            for quad in range(4):
                nc.sync.dma_start(
                    out=w_scales[32 * quad : 32 * quad + 4, side].bitcast(I32),
                    in_=scales[:, 4 * quad : 4 * quad + 4, :].rearrange("g r d -> r g d").bitcast(I32),
                )

        load_x(0)
        load_scales(Q_SIDE, q_w_scales)
        nc.sync.dma_start(out=bias_rows[0:8, :], in_=q_b.rearrange("h (t p) -> (h t) p", p=P))
        nc.sync.dma_start(out=bias_rows[8:16, :], in_=k_b.rearrange("h (t p) -> (h t) p", p=P))
        load_words(Q_SIDE, 0, q_w_words)
        load_words(Q_SIDE, 1, q_w_words)
        load_x(1)
        load_scales(K_SIDE, k_w_scales)
        load_words(K_SIDE, 0, k_w_words)
        load_words(K_SIDE, 1, k_w_words)
        for b in range(2, B):
            load_x(b)


        def bias_column(side, h):
            return (side * HEADS + h) * PACK


        def prepare_bias():
            bias_ps = gate_psum.tile([P, P], BF16, tag="gate")
            nc.tensor.transpose(bias_ps[:], bias_rows[:], identity[:])
            nc.vector.tensor_copy(out=bias[:], in_=bias_ps[:, 0 : 2 * HEADS * PACK])

        def negate_bias():
            first_q1 = bias_column(Q_SIDE, 1)
            nc.vector.tensor_scalar(
                out=minus_bias[:], in0=bias[:, first_q1 : first_q1 + PACK], scalar1=-1.0, scalar2=None, op0=ALU.mult
            )

        patch_grouped = {}
        patch_codes = {}
        patch_scales = {}
        planes = {}
        half_planes = {}

        def vector_tiles(b):
            return [0] if b in HALF else [0, 1]

        qk_grouped = {}
        qk_codes = {}
        qk_scales = {}
        sim_sbs = {}
        folds = {}
        diffs = {}
        atts = {}
        enhanceds = {}

        def interleave_on_scalar(words, rows):
            nc.scalar.copy(
                out=words.rearrange("p (c i) t -> p c t i", i=4),
                in_=rows.rearrange("p t (c i) -> p c t i", i=4),
            )

        def regroup_patch(b):
            grouped = stage.tile([P, N, PACK], BF16, align_bytes=64, tag="patch_grouped")
            interleave_on_scalar(grouped[:], x_sb[:, b])
            patch_grouped[b] = grouped

        def regroup_patch_halves(b):
            grouped = stage.tile([P, N, PACK], BF16, align_bytes=64, tag="patch_grouped")
            interleave_on_scalar(grouped[:, :P, :], x_sb[:, b, :, :P])
            nc.vector.tensor_copy(
                out=grouped[:, P:, :].rearrange("p (c i) t -> p c t i", i=4),
                in_=x_sb[:, b, :, P:].rearrange("p t (c i) -> p c t i", i=4),
            )
            patch_grouped[b] = grouped

        def quantise_patch(b):
            codes = stage.tile([P, N], U32, align_bytes=64, tag="patch_codes", bufs=3)
            scales = stage.tile([P, N], U8, align_bytes=64, tag="patch_scales", bufs=3)
            nc.vector.quantize_mx(
                out=codes[:].bitcast(FP8X4),
                scales=scales[:],
                in_=patch_grouped[b][:].rearrange("p n j -> p (n j)"),
            )
            patch_codes[b] = codes
            patch_scales[b] = scales

        def project_pass(out, b, side, h, t, n_cols):
            d_cols = slice(t * P, (t + 1) * P)
            nc.tensor.matmul_mx(
                out=out,
                lhsT=w_words[:, side, h, d_cols].bitcast(FP8X4),
                lhsT_scale=w_scales[:, side, h, d_cols],
                rhs=patch_codes[b][:, n_cols].bitcast(FP8X4),
                rhs_scale=patch_scales[b][:, n_cols],
                start=True,
                stop=True,
            )

        def open_batch(b):
            grouped = stage.tile([P, 2, HEADS, N, PACK], BF16, align_bytes=64, tag="qk_grouped")
            qk_grouped[b] = grouped

        def project_for_scalar(b):
            rows = stage.tile([P, PACK, N], BF16, tag="planes")
            planes[b] = rows
            for half in range(2):
                acc = planes_psum.tile([P, 2, N], F32, tag="planes_acc")
                for i in range(2):
                    project_pass(acc[:, i, :], b, Q_SIDE, 1, 2 * half + i, slice(0, N))
                for i in range(2):
                    t = 2 * half + i
                    nc.scalar.activation(
                        out=rows[:, t, :],
                        in_=acc[:, i, :],
                        func=ACT.Identity,
                        bias=minus_bias[:, t : t + 1],
                        scale=-1.0,
                    )

        def regroup_planes(b):
            if b > 0:
                interleave_on_scalar(qk_grouped[b][:, Q_SIDE, 1], planes[b][:])

        def regroup_half(b):
            interleave_on_scalar(qk_grouped[b][:, K_SIDE, 1, P:, :], half_planes[b][:])

        def project_half_for_scalar(b, side, h, nt):
            rows = stage.tile([P, PACK, P], BF16, tag="half_planes")
            half_planes[b] = rows
            first = bias_column(side, h)
            n_cols = slice(nt * P, (nt + 1) * P)
            acc = planes_psum.tile([P, PACK, P], F32, tag="planes_acc")
            for t in range(PACK):
                project_pass(acc[:, t, :], b, side, h, t, n_cols)
            for t in range(PACK):
                nc.scalar.activation(
                    out=rows[:, t, :],
                    in_=acc[:, t, :],
                    func=ACT.Identity,
                    bias=bias[:, first + t : first + t + 1],
                    scale=1.0,
                )

        def project_for_vector(b, side, h, tiles=range(N_TILES)):
            first = bias_column(side, h)
            for nt in tiles:
                n_cols = slice(nt * P, (nt + 1) * P)
                acc = proj_psum.tile([P, PACK, P], F32, tag="proj")
                for t in range(PACK):
                    project_pass(acc[:, t, :], b, side, h, t, n_cols)
                words = qk_grouped[b][:, side, h, n_cols, :]
                rows = acc[:].rearrange("p t n -> p n t")
                bias_words = bias[:, first : first + PACK].unsqueeze(1).to_broadcast([P, P, PACK])
                if (side, h) == (Q_SIDE, 1):
                    nc.vector.scalar_tensor_tensor(
                        out=words, in0=rows, scalar=-1.0, in1=bias_words, op0=ALU.mult, op1=ALU.subtract
                    )
                else:
                    nc.vector.tensor_tensor(out=words, in0=rows, in1=bias_words, op=ALU.add)

        def open_codes(b, side):
            codes = stage.tile([P, HEADS, N], U32, align_bytes=64, tag="qk_codes", bufs=4)
            scales = stage.tile([P, HEADS, N], U8, align_bytes=64, tag="qk_scales", bufs=4)
            qk_codes[b, side] = codes
            qk_scales[b, side] = scales

        def quantise_head(b, side, h):
            nc.vector.quantize_mx(
                out=qk_codes[b, side][:, h, :].bitcast(FP8X4),
                scales=qk_scales[b, side][:, h, :],
                in_=qk_grouped[b][:, side, h].rearrange("p n t -> p (n t)"),
            )

        def quantise_side(b, side):
            open_codes(b, side)
            codes = qk_codes[b, side]
            scales = qk_scales[b, side]
            nc.vector.quantize_mx(
                out=codes[:].rearrange("p h n -> p (h n)").bitcast(FP8X4),
                scales=scales[:].rearrange("p h n -> p (h n)"),
                in_=qk_grouped[b][:, side].rearrange("p h n t -> p (h n t)"),
            )

        def similarity_pass(out, b, h, qt, start, stop):
            q_cols = slice(qt * P, (qt + 1) * P)
            nc.tensor.matmul_mx(
                out=out,
                lhsT=qk_codes[b, Q_SIDE][:, h, q_cols].bitcast(FP8X4),
                lhsT_scale=qk_scales[b, Q_SIDE][:, h, q_cols],
                rhs=qk_codes[b, K_SIDE][:, h, :].bitcast(FP8X4),
                rhs_scale=qk_scales[b, K_SIDE][:, h, :],
                start=start,
                stop=stop,
            )

        def fold(b):
            folded_ps = planes_psum.tile([P, 2, N], F32, tag="planes_acc")
            out = folded_ps[:, 0, :]
            for h in range(HEADS):
                for qt in range(N_TILES):
                    similarity_pass(
                        out, b, h, qt,
                        start=(h == 0 and qt == 0),
                        stop=(h == HEADS - 1 and qt == N_TILES - 1),
                    )
            folded = results.tile([P, N], F32, tag="folded", bufs=2)
            nc.scalar.activation(out=folded[:], in_=out, func=ACT.Copy, scale=INV_SQRT_HD)
            folds[b] = folded

        def sum_fold(b):
            diff = gate_psum.tile([P, N], F32, tag="gate")
            diffs[b] = diff
            nc.tensor.matmul(out=diff[:], lhsT=plus_ones[:], rhs=folds[b][:], start=True, stop=True)

        def similarity(b):
            sim_sb = results.tile([P, HEADS, N_TILES, N], F32, tag="sim_sb")
            for h in range(HEADS):
                scale = INV_SQRT_HD if h == 0 else -INV_SQRT_HD
                sim_ps = sim_psum.tile([P, N_TILES, N], F32, tag="sim")
                for qt in range(N_TILES):
                    similarity_pass(sim_ps[:, qt, :], b, h, qt, start=True, stop=True)
                nc.scalar.activation(out=sim_sb[:, h], in_=sim_ps[:], func=ACT.Copy, scale=scale)
            sim_sbs[b] = sim_sb
            if b < LAST:
                store_similarity(b)

        def store_similarity(b):
            nc.sync.dma_start(out=out_2[b].rearrange("h (qt p) k -> p h qt k", p=P), in_=sim_sbs[b][:])

        def sum_queries(b, h):
            if h == 0:
                diff = gate_psum.tile([P, N], F32, tag="gate")
                diffs[b] = diff
            for qt in range(N_TILES):
                nc.tensor.matmul(
                    out=diffs[b][:],
                    lhsT=(plus_ones if h == 0 else minus_ones)[:],
                    rhs=sim_sbs[b][:, h, qt, :],
                    start=(h == 0 and qt == 0),
                    stop=(h == HEADS - 1 and qt == N_TILES - 1),
                )

        def gate(b):
            att = results.tile([P, HEADS, N], F32, tag="att", bufs=4)
            nc.scalar.activation(out=att[:, 0, :], in_=diffs[b][:], func=ACT.Sigmoid, scale=1.0)
            nc.scalar.activation(out=att[:, 1, :], in_=diffs[b][:], func=ACT.Sigmoid, scale=-1.0)
            atts[b] = att

        def store_gate(b):
            nc.sync.dma_start(
                out=out_0[b : b + 1].rearrange("o h i w -> o (h i w)"),
                in_=atts[b][0:1].rearrange("o h n -> o (h n)"),
            )

        def split_rows(b):
            return PACK - VECTOR_ROWS_OF.get(b, VECTOR_ROWS)

        def enhance_on_gpsimd(b):
            split = split_rows(b)
            enhanced = results.tile([P, HEADS, PACK, N], F32, tag="enhanced", bufs=6)
            enhanceds[b] = enhanced
            for h in range(HEADS):
                nc.gpsimd.tensor_tensor(
                    out=enhanced[:, h, :split, :],
                    in0=x_sb[:, b, :split, :],
                    in1=atts[b][:, h, :].unsqueeze(1).to_broadcast([P, split, N]),
                    op=ALU.mult,
                )

        def store_rows(b, first, end):
            nc.sync.dma_start(
                out=out_1[b].rearrange("(h p j) i w -> p h j (i w)", h=HEADS, j=PACK)[:, :, first:end, :],
                in_=enhanceds[b][:, :, first:end, :],
            )

        def store_gpsimd_rows(b, h):
            nc.sync.dma_start(
                out=out_1[b].rearrange("(h p j) i w -> p h j (i w)", h=HEADS, j=PACK)[:, h, : split_rows(b), :],
                in_=enhanceds[b][:, h, : split_rows(b), :],
            )

        def enhance_on_vector(b):
            split = split_rows(b)
            nc.vector.tensor_tensor(
                out=enhanceds[b][:, :, split:, :],
                in0=x_sb[:, b, split:, :].unsqueeze(1).to_broadcast([P, HEADS, PACK - split, N]),
                in1=atts[b][:].unsqueeze(2).to_broadcast([P, HEADS, PACK - split, N]),
                op=ALU.mult,
            )
            store_rows(b, split if b in LATE else 0, PACK)

        def enhance_by_heads(b):
            enhanced = results.tile([P, HEADS, PACK, N], F32, tag="enhanced", bufs=6)
            rows = out_1[b].rearrange("(h p j) i w -> p h j (i w)", h=HEADS, j=PACK)
            for h in range(HEADS):
                parts = [slice(0, 2), slice(2, 4)] if (b, h) == (LAST, 1) else [slice(0, 4)]
                for j in parts:
                    nc.vector.tensor_tensor(
                        out=enhanced[:, h, j],
                        in0=x_sb[:, b, j],
                        in1=atts[b][:, h, :].unsqueeze(1).to_broadcast([P, j.stop - j.start, N]),
                        op=ALU.mult,
                    )
                    nc.sync.dma_start(out=rows[:, h, j], in_=enhanced[:, h, j])

        def keep_tensor_warm(passes, rhs):
            idle = planes_psum.tile([P, 2 * N], F32, tag="planes_acc")
            for i in range(passes):
                nc.tensor.matmul(
                    out=idle[:, : rhs.shape[1]], lhsT=identity[:], rhs=rhs, start=True, stop=True
                )

        regroup_patch_halves(0)
        quantise_patch(0)
        keep_tensor_warm(24, identity[:])
        prepare_bias()
        open_batch(0)
        regroup_patch(1)
        for b in range(LAST):
            project_for_vector(b, Q_SIDE, 0)
            if b == 0:
                project_for_vector(0, Q_SIDE, 1)
            if b > 0:
                similarity(b - 1)
                regroup_planes(b)
            project_for_vector(b, K_SIDE, 0)
            if 1 <= b and b + 2 < B:
                regroup_patch(b + 2)
            open_batch(b + 1)
            if b > 0:
                project_for_scalar(b + 1)
            project_for_vector(b, K_SIDE, 1, tiles=vector_tiles(b))
            if b == 0:
                if 0 in HALF:
                    project_half_for_scalar(0, K_SIDE, 1, 1)
                    regroup_half(0)
                regroup_patch(2)
                quantise_patch(1)
                negate_bias()
                project_for_scalar(1)
            if b > 0:
                sum_queries(b - 1, 0)
                sum_queries(b - 1, 1)
                gate(b - 1)
            if b + 1 in HALF:
                project_half_for_scalar(b + 1, K_SIDE, 1, 1)
            quantise_side(b, Q_SIDE)
            quantise_side(b, K_SIDE)
            if b >= 1:
                enhance_on_gpsimd(b - 1)
            if b >= 2 and b - 2 not in LATE:
                enhance_on_vector(b - 2)
            if b >= 1:
                store_gate(b - 1)
            if b + 2 < B:
                quantise_patch(b + 2)

        regroup_planes(LAST)
        project_for_vector(LAST, Q_SIDE, 0)
        project_for_vector(LAST, K_SIDE, 0, tiles=[0])
        fold(LAST - 1)
        store_gpsimd_rows(LAST - 2, 0)
        project_for_vector(LAST, K_SIDE, 0, tiles=[1])
        similarity(LAST - 1)
        regroup_half(LAST)
        store_gpsimd_rows(LAST - 2, 1)
        project_for_vector(LAST, K_SIDE, 1, tiles=vector_tiles(LAST))
        sum_fold(LAST - 1)
        keep_tensor_warm(4, x_sb[:, LAST, 0:2, :].rearrange("p j n -> p (j n)"))
        gate(LAST - 1)
        quantise_side(LAST, Q_SIDE)
        quantise_side(LAST, K_SIDE)
        enhance_on_vector(LAST - 2)
        store_gate(LAST - 1)
        fold(LAST)
        similarity(LAST)
        sum_fold(LAST)
        gate(LAST)
        enhance_by_heads(LAST - 1)
        store_similarity(LAST)
        store_gate(LAST)
        enhance_by_heads(LAST)
